import numpy as np
import ml_dtypes


def mxq(x, axis, fmt="e4m3"):
    dtype, down = {"e4m3": (ml_dtypes.float8_e4m3fn, 7), "e5m2": (ml_dtypes.float8_e5m2, 14)}[fmt]
    v = np.moveaxis(np.asarray(x, np.float32).astype(ml_dtypes.bfloat16).astype(np.float64), axis, -1)
    blocks = v.reshape(v.shape[:-1] + (-1, 32))
    amax = np.abs(blocks).max(-1, keepdims=True)
    byte = np.maximum(np.where(amax > 0, np.frexp(amax)[1] - 1 + 127, 0) - down, 1)
    scale = np.exp2(byte - 127.0)
    codes = (blocks / scale).astype(np.float32).astype(dtype).astype(np.float64)
    return np.moveaxis((codes * scale).reshape(v.shape), -1, axis)


WIDE = False


def mx_kscale(k):
    if not WIDE:
        return np.ones(k)
    levels = np.array([10, -10, 5, -5, 0])
    if k % 512:
        return np.exp2(np.random.permutation(np.resize(levels, k // 32))).repeat(32)
    a = np.empty((k // 512, 16))
    for p in range(k // 512):
        a[p, :8] = np.random.permutation(np.resize(levels, 8))
        for g in range(8):
            far = levels[np.abs(levels - a[p, g]) >= 10]
            a[p, g + 8] = far[np.random.randint(len(far))]
    return np.exp2(a.ravel()).repeat(32)


BF16 = ml_dtypes.bfloat16


def bf(x):
    return np.asarray(x, np.float32).astype(BF16)


def f64(x):
    return np.asarray(x).astype(np.float64)


E2M1 = np.array([0.0, 0.5, 1.0, 1.5, 2.0, 3.0, 4.0, 6.0, -0.0, -0.5, -1.0, -1.5, -2.0, -3.0, -4.0, -6.0])


def pack_weight(w, fmt):
    k, n = w.shape
    w = f64(bf(w)).reshape(k // 32, 32, n)
    amax = np.abs(w).max(1)
    if fmt == "e4m3":
        byte = np.frexp(amax)[1] - 1 + 127 - 7
    else:
        mant, ex = np.frexp(amax / 6.0)
        byte = np.where(mant > 0.5, ex, ex - 1) + 127
    byte = np.clip(np.where(amax > 0, byte, 1), 1, 254)
    scaled = (w * np.exp2(127.0 - byte)[:, None, :]).reshape(k, n).astype(np.float32)
    by_word = np.ascontiguousarray(scaled.reshape(k // 512, 128, 4, n).transpose(0, 1, 3, 2))
    if fmt == "e4m3":
        words = by_word.astype(ml_dtypes.float8_e4m3fn).view(np.uint8)
    else:
        c = by_word.astype(ml_dtypes.float4_e2m1fn).view(np.uint8) & 0xF
        words = c[..., 0::2] | (c[..., 1::2] << 4)
    return np.ascontiguousarray(words), np.ascontiguousarray(byte.astype(np.uint8).reshape(k // 512, 16, n))


def unpack_weight(words, scales, fmt):
    g, p, n, _ = words.shape
    if fmt == "e4m3":
        vals = np.ascontiguousarray(words).view(ml_dtypes.float8_e4m3fn).astype(np.float64)
    else:
        nib = np.empty((g, p, n, 4), np.uint8)
        nib[..., 0::2] = words & 0xF
        nib[..., 1::2] = words >> 4
        vals = E2M1[nib]
    vals = vals * np.repeat(np.exp2(scales.astype(np.float64) - 127.0), 8, axis=1)[..., None]
    return vals.transpose(0, 1, 3, 2).reshape(g * 512, n)
def pack4(w):
    words, scales = pack_weight(w, "e2m1")
    return words.reshape(words.shape[0], 128, -1), scales


def unpack4(words, scales):
    return unpack_weight(words.reshape(words.shape[0], 128, -1, 2), scales, "e2m1")


B, T, D, H, DK, ROPE, NOPE, VD, KVR, QR = 1, 8192, 512, 2, 128, 64, 64, 128, 512, 1024
EPS = 1.1920928955078125e-07
HALF = ROPE // 2


def rms_norm(h, w):
    var = np.mean(h * h, axis=-1, keepdims=True)
    return h * (1.0 / np.sqrt(var + EPS)) * w


def rope(v):
    inv_freq = 1.0 / (10000.0 ** (f64(np.arange(0, ROPE, 2)) / ROPE))
    freqs = np.outer(f64(np.arange(v.shape[-2])), inv_freq)
    cos, sin = np.cos(freqs), np.sin(freqs)
    v1, v2 = v[..., :HALF], v[..., HALF:]
    return np.concatenate([v1 * cos - v2 * sin, v1 * sin + v2 * cos], axis=-1)


def draw0():
    s, t = mx_kscale(D), mx_kscale(KVR)
    x = bf(np.random.standard_normal((B, T, D)) * s)
    wkv_c_words, wkv_c_scales = pack4(np.random.standard_normal((D, KVR)) / np.sqrt(D) / s[:, None])
    kv_a_norm_w = bf((1.0 + 0.1 * np.random.standard_normal(KVR)) * t)
    wkv_b_words, wkv_b_scales = pack4(np.random.standard_normal((KVR, H * (NOPE + VD))) / np.sqrt(KVR) / t[:, None])
    return {'x': x,
            'wkv_c_words': wkv_c_words,
            'wkv_c_scales': wkv_c_scales,
            'kv_a_norm_w': kv_a_norm_w,
            'wkv_b_words': wkv_b_words,
            'wkv_b_scales': wkv_b_scales,
            'k_pe': bf(np.random.standard_normal((B, T, ROPE)))}


def core(x, wkv_c_words, wkv_c_scales, kv_a_norm_w, wkv_b_words, wkv_b_scales, k_pe):
    c = mxq(f64(x), 2, 'e4m3') @ unpack4(wkv_c_words, wkv_c_scales)
    cn = rms_norm(c, f64(kv_a_norm_w))
    kv = mxq(cn, 2, 'e4m3') @ unpack4(wkv_b_words, wkv_b_scales)
    kv = kv.reshape(B, T, H, NOPE + VD).transpose(0, 2, 1, 3)
    k_nope, v = kv[..., :NOPE], kv[..., NOPE:]
    k_rot = rope(f64(k_pe)[:, None])
    k_rot = np.broadcast_to(k_rot, (B, H, T, ROPE))
    ks = np.concatenate([k_nope, k_rot], axis=-1)
    return ks, np.ascontiguousarray(v)


def e4m3fn_bytes(y):
    return np.clip(np.asarray(y, np.float64), -448.0, 448.0).astype(np.float32).astype(ml_dtypes.float8_e4m3fn).view(np.uint8)


def e4m3fn_values(b):
    return np.asarray(b, np.uint8).view(ml_dtypes.float8_e4m3fn).astype(np.float64)


def setup_inputs():
    d = draw0()
    x0 = np.asarray(d['x']).astype(np.float64)
    s = (np.max(np.abs(x0), axis=(0, 1), keepdims=True) / 448.0).astype(np.float32)
    out = {}
    for k, v in d.items():
        if k == 'x':
            out['x_bytes'] = e4m3fn_bytes(x0 / s.astype(np.float64))
            out['x_scale'] = s
        else:
            out[k] = v
    return out


def reference(x_bytes, x_scale, wkv_c_words, wkv_c_scales, kv_a_norm_w, wkv_b_words, wkv_b_scales, k_pe):
    return core(e4m3fn_values(x_bytes) * x_scale.astype(np.float64), wkv_c_words, wkv_c_scales, kv_a_norm_w, wkv_b_words, wkv_b_scales, k_pe)

@@ -1,0 +1,486 @@
+import math
+from contextlib import ExitStack
+
+import concourse.mybir as mybir
+from concourse.masks import make_identity
+
+F32 = mybir.dt.float32
+BF16 = mybir.dt.bfloat16
+I32 = mybir.dt.int32
+U32 = mybir.dt.uint32
+U8 = mybir.dt.uint8
+FP8 = mybir.dt.float8_e4m3fn
+FP8X4 = mybir.dt.float8_e4m3fn_x4
+FP4X4 = mybir.dt.float4_e2m1fn_x4
+ALU = mybir.AluOpType
+ACT = mybir.ActivationFunctionType
+
+P = 128
+TOKENS, DIM, LATENT = 8192, 512, 512
+HEADS, NOPE, ROPE, VDIM = 2, 64, 64, 128
+HALF = ROPE // 2
+EPS = 2.0**-23
+TILES = TOKENS // P
+PAIRS = TILES // 2
+GROUP = 8
+GROUPS = TILES // GROUP
+KV = HEADS * (NOPE + VDIM)
+FLOPS = 2 * TOKENS * DIM * (LATENT + KV)
+
+
+def tile_deepseekmultiheadattention_pb_t_w4_kernel(
+    tc, x_bytes, x_scale, wkv_c_words, wkv_c_scales, kv_a_norm_w, wkv_b_words, wkv_b_scales, k_pe, out_0, out_1
+):
+    nc = tc.nc
+    with ExitStack() as ctx:
+        const = ctx.enter_context(tc.tile_pool(name="const", bufs=1))
+        work = ctx.enter_context(tc.tile_pool(name="work", bufs=5))
+        outs = ctx.enter_context(tc.tile_pool(name="outs", bufs=3))
+        psum = ctx.enter_context(tc.psum_pool(name="psum", bufs=1))
+        ctx.enter_context(tc.manual_schedule())
+
+        ones = const.tile([P, 1], F32)
+        nc.vector.memset(ones[:], 1.0)
+        warm = const.tile([P, 1], F32)
+        nc.scalar.activation(out=warm[:], in_=ones[:], func=ACT.Sin)
+        wc_scale_rows = const.tile([P, LATENT], U8, align_bytes=64)
+        nc.vector.memset(wc_scale_rows[:].bitcast(I32), 0)
+        wb_scale_rows = const.tile([P, KV], U8, align_bytes=64)
+        nc.vector.memset(wb_scale_rows[:].bitcast(I32), 0)
+
+        xb = const.tile([P, TILES, DIM], U8)
+        x_rows = x_bytes[0].rearrange("(p i) k -> p i k", p=P)
+
+        def load_x(a, b):
+            nc.sync.dma_start(out=xb[:, a:b, :], in_=x_rows[:, a:b, :])
+
+        load_x(0, 2)
+        scale2 = const.tile([P, 2, DIM], F32)
+        nc.sync.dma_start(out=scale2[:, 0, :], in_=x_scale.rearrange("a b k -> (a b k)").partition_broadcast(P))
+        wc_nat = const.tile([P, 2 * LATENT], U8, align_bytes=64)
+        nc.sync.dma_start(out=wc_nat[:].bitcast(I32), in_=wkv_c_words[0].bitcast(I32))
+        for r in range(4):
+            nc.sync.dma_start(out=wc_scale_rows[r:P:32, :].bitcast(I32), in_=wkv_c_scales[0][r:16:4, :].bitcast(I32))
+        load_x(2, 8)
+        gain_nat = const.tile([P, LATENT], BF16)
+        nc.sync.dma_start(out=gain_nat[:], in_=kv_a_norm_w.partition_broadcast(P))
+        wb = const.tile([P, 2 * KV], U8, align_bytes=64)
+        wb_in = wkv_b_words[0].bitcast(I32).rearrange("p (h c) -> p h c", h=HEADS)
+        wb_out = wb[:].bitcast(I32)
+        nc.sync.dma_start(out=wb_out[:, 0:128].rearrange("p (h c) -> p h c", h=HEADS), in_=wb_in[:, :, 32:96])
+        nc.sync.dma_start(out=wb_out[:, 128:192].rearrange("p (h c) -> p h c", h=HEADS), in_=wb_in[:, :, 0:32])
+        for r in range(4):
+            nc.sync.dma_start(out=wb_scale_rows[r:P:32, :].bitcast(I32), in_=wkv_b_scales[0][r:16:4, :].bitcast(I32))
+        load_x(8, 16)
+        kp = const.tile([P, TILES, ROPE], BF16)
+        kp_rows = k_pe[0].rearrange("(p i) c -> p i c", p=P)
+        nc.sync.dma_start(out=kp[:, 0:16, :], in_=kp_rows[:, 0:16, :])
+        load_x(16, 24)
+        nc.sync.dma_start(out=kp[:, 16:TILES, :], in_=kp_rows[:, 16:TILES, :])
+        for a in range(24, TILES, 8):
+            load_x(a, a + 8)
+
+        pcol = const.tile([P, 1], F32)
+        nc.gpsimd.iota(pcol[:], [[0, 1]], base=0, channel_multiplier=1, allow_small_or_imprecise_dtypes=True)
+        eights = const.tile([P, GROUPS], F32)
+        nc.gpsimd.iota(
+            eights[:], [[GROUP, GROUPS]], base=0, channel_multiplier=0, allow_small_or_imprecise_dtypes=True
+        )
+        ident = const.tile([P, P], F32)
+        make_identity(nc, ident[:])
+        neg_half = const.tile([P, 2], F32)
+        nc.gpsimd.memset(neg_half[:], -0.5)
+        late = const.tile([P, 1], F32)
+        nc.gpsimd.tensor_scalar(out=late[:], in0=pcol[:], scalar1=64.0, scalar2=None, op0=ALU.is_ge)
+        t64 = const.tile([P, 1], F32)
+        nc.gpsimd.tensor_scalar(out=t64[:], in0=late[:], scalar1=-64.0, scalar2=0.0, op0=ALU.mult, op1=ALU.add)
+        xi = const.tile([P, 1], F32)
+        nc.gpsimd.tensor_tensor(out=xi[:], in0=pcol[:], in1=t64[:], op=ALU.add)
+        ph0 = const.tile([P, 1], F32)
+        nc.gpsimd.tensor_scalar(out=ph0[:], in0=late[:], scalar1=-0.25, scalar2=0.25, op0=ALU.mult, op1=ALU.add)
+        sg1 = const.tile([P, 1], F32)
+        nc.gpsimd.tensor_scalar(out=sg1[:], in0=late[:], scalar1=2.0, scalar2=-1.0, op0=ALU.mult, op1=ALU.add)
+        xs = const.tile([P, 1], F32)
+        nc.gpsimd.tensor_tensor(out=xs[:], in0=xi[:], in1=sg1[:], op=ALU.mult)
+        ph1 = const.tile([P, 1], F32)
+        nc.gpsimd.tensor_scalar(out=ph1[:], in0=late[:], scalar1=0.25, scalar2=0.0, op0=ALU.mult, op1=ALU.add)
+
+        ratio = 10000.0 ** (-1.0 / HALF)
+        freq = const.tile([P, HALF], F32)
+        turn64 = const.tile([P, HALF], F32)
+        nc.vector.tensor_scalar(
+            out=freq[:, 0:1], in0=ones[:], scalar1=1.0 / (2.0 * math.pi), scalar2=None, op0=ALU.mult
+        )
+        filled = 1
+        for j in range(HALF):
+            turns = 64.0 * ratio**j / (2.0 * math.pi)
+            turns = turns - round(turns)
+            if j % 3 == 2:
+                nc.scalar.activation(out=turn64[:, j : j + 1], in_=ones[:], func=ACT.Copy, scale=turns)
+            else:
+                nc.vector.tensor_scalar(
+                    out=turn64[:, j : j + 1], in0=ones[:], scalar1=turns, scalar2=None, op0=ALU.mult
+                )
+            if j % 4 == 3 and filled < HALF:
+                nc.vector.tensor_scalar(
+                    out=freq[:, filled : 2 * filled], in0=freq[:, 0:filled], scalar1=ratio**filled, scalar2=None,
+                    op0=ALU.mult,
+                )
+                filled *= 2
+        step8 = const.tile([P, GROUPS, HALF], F32)
+        nc.vector.tensor_tensor(
+            out=step8[:],
+            in0=freq[:].unsqueeze(1).to_broadcast([P, GROUPS, HALF]),
+            in1=eights[:].unsqueeze(2).to_broadcast([P, GROUPS, HALF]),
+            op=ALU.mult,
+        )
+        base = const.tile([P, HALF], F32)
+        nc.vector.tensor_scalar(out=base[:], in0=turn64[:], scalar1=pcol[:], scalar2=None, op0=ALU.mult)
+
+        x_bf, x_grp, x_cod, x_scl = {}, {}, {}, {}
+        c_ps, rms, cn_bf, cn_cod, cn_scl = {}, {}, {}, {}, {}
+        v_ps, n_ps, v_sb, ks_sb = {}, {}, {}, {}
+        t_ps, ss_sb = {}, {}
+
+        def widen(j):
+            xw = work.tile([P, 2, DIM], BF16, name="xw")
+            x_bf[j] = xw
+            if j == 0:
+                for t in range(2):
+                    nc.vector.tensor_tensor(
+                        out=xw[:, t, :], in0=xb[:, t, :].bitcast(FP8), in1=scale2[:, 0, :], op=ALU.mult
+                    )
+            else:
+                nc.vector.tensor_tensor(
+                    out=xw[:].rearrange("p a k -> p (a k)"),
+                    in0=xb[:, 2 * j : 2 * j + 2, :].rearrange("p a k -> p (a k)").bitcast(FP8),
+                    in1=scale2[:].rearrange("p a k -> p (a k)"),
+                    op=ALU.mult,
+                )
+
+        def transpose_x(j):
+            bank = psum.tile([P, 2, 2, P], F32, name="xt", tag="t", bufs=2)
+            t_ps["x", j] = bank
+            for t in range(2):
+                words = x_bf[j][:, t, :].bitcast(F32)
+                for u in range(2):
+                    nc.tensor.transpose(bank[:, t, u, :], words[:, u:256:2], ident[:])
+
+        def copy_x(j):
+            xg = work.tile([P, 8 * P], BF16, name="xg", align_bytes=64)
+            x_grp[j] = xg
+            nc.scalar.copy(
+                out=xg[:].bitcast(F32).rearrange("p (a r u) -> p a r u", a=2, u=2),
+                in_=t_ps["x", j][:].rearrange("p a u r -> p a r u"),
+            )
+
+        def quant_x(j):
+            cod = work.tile([P, 2 * P], U32, name="xq", align_bytes=64)
+            scl = work.tile([P, 2 * P], U8, name="xqs", align_bytes=64)
+            x_cod[j], x_scl[j] = cod, scl
+            nc.vector.quantize_mx(out=cod[:].bitcast(FP8X4), scales=scl[:], in_=x_grp[j][:])
+
+        def latent(j, t):
+            bank = psum.tile([P, LATENT], F32, name="c", tag="c", bufs=3)
+            c_ps[j, t] = bank
+            cols = slice(t * P, (t + 1) * P)
+            nc.tensor.matmul_mx(
+                out=bank[:],
+                lhsT=x_cod[j][:, cols].bitcast(FP8X4),
+                lhsT_scale=x_scl[j][:, cols],
+                rhs=wc[:].bitcast(FP4X4),
+                rhs_scale=wcs[:],
+                start=True,
+                stop=True,
+            )
+
+        def squares(j, t):
+            if t == 0:
+                ss_sb[j] = work.tile([P, 2], F32, name="ss")
+            junk = work.tile([P, LATENT], BF16, name="junk", bufs=2)
+            nc.scalar.activation(out=junk[:], in_=c_ps[j, t][:], func=ACT.Square, accum_out=ss_sb[j][:, t : t + 1])
+
+        def inverse_rms(j):
+            ss = ss_sb[j]
+            ms = work.tile([P, 2], F32, name="ms")
+            nc.gpsimd.tensor_scalar(out=ms[:], in0=ss[:], scalar1=1.0 / LATENT, scalar2=EPS, op0=ALU.mult, op1=ALU.add)
+            rs = work.tile([P, 2], F32, name="rs")
+            nc.gpsimd.tensor_tensor(out=rs[:], in0=ms[:], in1=neg_half[:], op=ALU.pow)
+            rms[j] = rs
+
+        def normalise(j, t):
+            if t == 0:
+                cn_bf[j] = work.tile([P, 2, LATENT], BF16, name="cn")
+            nc.vector.scalar_tensor_tensor(
+                out=cn_bf[j][:, t, :],
+                in0=c_ps[j, t][:],
+                scalar=rms[j][:, t : t + 1],
+                in1=gain[:],
+                op0=ALU.mult,
+                op1=ALU.mult,
+            )
+
+        def transpose_cn(j):
+            bank = psum.tile([P, 2, 2, P], F32, name="ct", tag="t", bufs=2)
+            t_ps["c", j] = bank
+            for t in range(2):
+                words = cn_bf[j][:, t, :].bitcast(F32)
+                for u in range(2):
+                    nc.tensor.transpose(bank[:, t, u, :], words[:, u * P : (u + 1) * P], ident[:])
+
+        def copy_cn(j):
+            cg = work.tile([P, 8 * P], BF16, name="cg", align_bytes=64)
+            cn_bf[j] = cg
+            nc.scalar.copy(
+                out=cg[:].bitcast(F32).rearrange("p (a r u) -> p a r u", a=2, u=2),
+                in_=t_ps["c", j][:].rearrange("p a u r -> p a r u"),
+            )
+
+        def quant_cn(j):
+            cod = work.tile([P, 2 * P], U32, name="cq", align_bytes=64)
+            scl = work.tile([P, 2 * P], U8, name="cqs", align_bytes=64)
+            cn_cod[j], cn_scl[j] = cod, scl
+            nc.vector.quantize_mx(out=cod[:].bitcast(FP8X4), scales=scl[:], in_=cn_bf[j][:])
+
+        def expand(j):
+            v_ps[j] = psum.tile([P, 2, HEADS * VDIM], F32, name="v", tag="v")
+            if j % 2 == 0:
+                n_ps[j // 2] = psum.tile([P, 4, HEADS * NOPE], F32, name="n", tag="n")
+            for t in range(2):
+                cols = slice(t * P, (t + 1) * P)
+                left = cn_cod[j][:, cols].bitcast(FP8X4)
+                left_scale = cn_scl[j][:, cols]
+                nc.tensor.matmul_mx(
+                    out=v_ps[j][:, t, :],
+                    lhsT=left,
+                    lhsT_scale=left_scale,
+                    rhs=wb[:, 0:512].bitcast(FP4X4),
+                    rhs_scale=wbs[:, 0:256],
+                    start=True,
+                    stop=True,
+                )
+                nc.tensor.matmul_mx(
+                    out=n_ps[j // 2][:, 2 * (j % 2) + t, :],
+                    lhsT=left,
+                    lhsT_scale=left_scale,
+                    rhs=wb[:, 512:768].bitcast(FP4X4),
+                    rhs_scale=wbs[:, 256:384],
+                    start=True,
+                    stop=True,
+                )
+
+        def ks_tile(g):
+            if g not in ks_sb:
+                ks_sb[g] = outs.tile([P, GROUP, 3 * ROPE], F32, name="ks")
+            return ks_sb[g]
+
+        def copy_v(j):
+            q = j // 2
+            if j % 2 == 0:
+                v_sb[q] = outs.tile([P, HEADS, 4, VDIM], F32, name="vo")
+            a = 2 * (j % 2)
+            nc.scalar.copy(
+                out=v_sb[q][:, :, a : a + 2, :].rearrange("p h i c -> p i h c"),
+                in_=v_ps[j][:].rearrange("p i (h c) -> p i h c", h=HEADS),
+            )
+            v_rows = out_1[0].rearrange("h (p i) c -> p h i c", p=P)
+            if q == PAIRS // 2 - 1:
+                nc.sync.dma_start(
+                    out=v_rows[:, :, 2 * j : 2 * j + 2, :], in_=v_sb[q][:, :, a : a + 2, :]
+                )
+            elif j % 2 == 1:
+                nc.sync.dma_start(out=v_rows[:, :, 4 * q : 4 * q + 4, :], in_=v_sb[q][:])
+
+        def store_ks(q):
+            b = 4 * (q % 2)
+            ks = ks_tile(q // 2)[:, b : b + 4, :]
+            out0 = out_0[0, 0].rearrange("(p i) c -> p i c", p=P)[:, 4 * q : 4 * q + 4, :]
+            out1 = out_0[0, 1].rearrange("(p i) c -> p i c", p=P)[:, 4 * q : 4 * q + 4, :]
+            nc.sync.dma_start(out=out1, in_=ks[:, :, NOPE : 3 * NOPE])
+            nc.sync.dma_start(out=out0[:, :, 0:NOPE], in_=ks[:, :, 0:NOPE])
+            nc.sync.dma_start(out=out0[:, :, NOPE:], in_=ks[:, :, 2 * NOPE :])
+
+        def copy_nope(j):
+            if j % 2 == 1:
+                q = j // 2
+                b = 4 * (q % 2)
+                nc.scalar.copy(out=ks_tile(q // 2)[:, b : b + 4, 0 : 2 * NOPE], in_=n_ps[q][:])
+                have.add(q)
+                if q // 2 in turned:
+                    store_ks(q)
+
+        trig = const.tile([P, 640], F32)
+        trig_i = const.tile([P, 640], I32)
+        lt = const.tile([P, GROUPS, 4, HALF], BF16)
+        left_rot = const.tile([P, GROUPS, P], BF16)
+        ident_b = const.tile([P, P], BF16)
+        mask = const.tile([P, HALF], F32)
+        rot_hi = const.tile([P, 2 * GROUP * HALF], BF16)
+        rot_lo = const.tile([P, 2 * GROUP * HALF], BF16)
+        rot = const.tile([P, 2 * GROUP * HALF], F32)
+        short = const.tile([P, GROUP, 2], F32)
+
+        def angles():
+            u = trig[:, 0:512].rearrange("p (g q j) -> p g q j", g=GROUPS, q=2)
+            nc.vector.tensor_tensor(
+                out=u[:, :, 1, :], in0=step8[:], in1=base[:].unsqueeze(1).to_broadcast([P, GROUPS, HALF]), op=ALU.add
+            )
+            nc.vector.tensor_scalar(out=u[:, :, 0, :], in0=u[:, :, 1, :], scalar1=0.25, scalar2=None, op0=ALU.add)
+
+        def angles_2():
+            for q in range(4):
+                nc.vector.tensor_scalar(
+                    out=trig[:, 512 + HALF * q : 512 + HALF * (q + 1)],
+                    in0=freq[:],
+                    scalar1=(xs if q % 2 else xi)[:],
+                    scalar2=(ph1 if q % 2 else ph0)[:],
+                    op0=ALU.mult,
+                    op1=ALU.add,
+                )
+            nc.vector.tensor_copy(out=trig_i[:], in_=trig[:])
+            nc.vector.tensor_tensor(out=trig[:], in0=trig[:], in1=trig_i[:], op=ALU.subtract)
+            nc.scalar.activation(out=trig[:], in_=trig[:], func=ACT.Sin, scale=2.0 * math.pi)
+
+        def split_left():
+            s = trig[:, 0:512].rearrange("p (g q j) -> p g q j", g=GROUPS, q=2)
+            nc.vector.tensor_copy(out=ident_b[:], in_=ident[:])
+            nc.vector.tensor_copy(out=lt[:, :, 0:2, :], in_=s)
+            nc.vector.tensor_tensor(out=lt[:, :, 2:4, :], in0=s, in1=lt[:, :, 0:2, :], op=ALU.subtract)
+            nc.vector.tensor_reduce(
+                out=mask[:], in_=ident[:].rearrange("k (q j) -> k j q", q=4), axis=mybir.AxisListType.X, op=ALU.add
+            )
+
+        def turn_tables():
+            xt = psum.tile([P, P], F32, name="tx", tag="v")
+            nc.tensor.transpose(xt[:], trig[:, 512:640], ident[:])
+            bank = psum.tile([P, GROUPS, P], BF16, name="tl", tag="r")
+            for g in range(GROUPS):
+                nc.tensor.transpose(bank[:, g, :], lt[:, g, :, :].rearrange("p q j -> p (q j)"), ident_b[:])
+            nc.vector.tensor_copy(
+                out=short[:], in_=xt[:].rearrange("k (c i) -> k i c", c=2)[:, 0:GROUP, :]
+            )
+            nc.scalar.copy(out=left_rot[:], in_=bank[:])
+
+        def right_tables():
+            nc.vector.tensor_tensor(
+                out=rot[:].rearrange("k (i c j) -> k i c j", i=GROUP, c=2),
+                in0=short[:].unsqueeze(3).to_broadcast([P, GROUP, 2, HALF]),
+                in1=mask[:].unsqueeze(1).unsqueeze(1).to_broadcast([P, GROUP, 2, HALF]),
+                op=ALU.mult,
+            )
+            nc.vector.tensor_copy(out=rot_hi[:], in_=rot[:])
+            nc.vector.tensor_tensor(out=rot_lo[:], in0=rot[:], in1=rot_hi[:], op=ALU.subtract)
+
+        r_ps, m_sb = {}, {}
+        have, turned = set(), set()
+
+        def rotate_pe(g):
+            bank = psum.tile([P, GROUP, 2, HALF], F32, name="r", tag="r")
+            r_ps[g] = bank
+            flat = bank[:].rearrange("p i c j -> p (i c j)")
+            nc.tensor.matmul(flat, left_rot[:, g, :], rot_hi[:], start=True, stop=False)
+            nc.tensor.matmul(flat, left_rot[:, g, :], rot_lo[:], start=False, stop=True)
+
+        def rotate_step(j):
+            if j % 4 == 0:
+                rotate_pe(j // 4)
+            rotate(j // 4, j % 4)
+            if j % 4 == 3:
+                turned.add(j // 4)
+                for q in (j // 2 - 1, j // 2):
+                    if q in have:
+                        store_ks(q)
+
+        def rotate(g, phase):
+            kin = kp[:, GROUP * g : GROUP * (g + 1), :].rearrange("p i (h j) -> p i h j", h=2)
+            if phase < 2:
+                m = work.tile([P, GROUP, 2, HALF], F32, name="m%d" % phase, bufs=2)
+                m_sb[g, phase] = m
+                nc.vector.tensor_tensor(
+                    out=m[:],
+                    in0=kin,
+                    in1=r_ps[g][:, :, phase, :].unsqueeze(2).to_broadcast([P, GROUP, 2, HALF]),
+                    op=ALU.mult,
+                )
+            else:
+                other = phase == 2
+                ks = ks_tile(g)
+                c0 = 2 * NOPE + (0 if other else HALF)
+                nc.vector.tensor_tensor(
+                    out=ks[:, :, c0 : c0 + HALF],
+                    in0=m_sb[g, 0][:, :, 0 if other else 1, :],
+                    in1=m_sb[g, 1][:, :, 1 if other else 0, :],
+                    op=ALU.subtract if other else ALU.add,
+                )
+
+        wc = const.tile([P, 2 * LATENT], U8, align_bytes=64)
+        wcs = const.tile([P, LATENT], U8, align_bytes=64)
+        wbs = const.tile([P, KV], U8, align_bytes=64)
+        gain = const.tile([P, LATENT], BF16)
+
+        def latent_weights():
+            nc.vector.tensor_copy(
+                out=wc[:].bitcast(I32).rearrange("q (u p) -> q p u", u=2),
+                in_=wc_nat[:].bitcast(I32).rearrange("q (p u) -> q p u", u=2),
+            )
+            nc.vector.tensor_copy(
+                out=wcs[:].rearrange("q (u p e) -> q p u e", u=2, e=2),
+                in_=wc_scale_rows[:].rearrange("q (p u e) -> q p u e", u=2, e=2),
+            )
+
+        def gain_order():
+            nc.vector.tensor_copy(
+                out=gain[:].rearrange("q (u p e) -> q p u e", u=2, e=2),
+                in_=gain_nat[:].rearrange("q (p u e) -> q p u e", u=2, e=2),
+            )
+
+        def expand_weights():
+            rows = wb_scale_rows[:].rearrange("q (h c) -> q h c", h=HEADS)
+            nc.gpsimd.tensor_copy(
+                out=wbs[:, 0:256].rearrange("q (h c) -> q h c", h=HEADS), in_=rows[:, :, NOPE:]
+            )
+            nc.gpsimd.tensor_copy(
+                out=wbs[:, 256:384].rearrange("q (h c) -> q h c", h=HEADS), in_=rows[:, :, 0:NOPE]
+            )
+
+        steps = (
+            (widen, 4),
+            (latent, 2, 0),
+            (copy_x, 3),
+            (normalise, 1, 0),
+            (expand, -1),
+            (latent, 2, 1),
+            (normalise, 1, 1),
+            (transpose_cn, 1),
+            (squares, 2, 0),
+            (quant_cn, 0),
+            (quant_x, 3),
+            (rotate_step, 1),
+            (squares, 2, 1),
+            (copy_nope, -1),
+            (inverse_rms, 2),
+            (copy_v, -1),
+            (copy_cn, 1),
+            (transpose_x, 4),
+        )
+        for s in range(-4, PAIRS + 1):
+            if s == -4:
+                angles()
+            if s == -2:
+                turn_tables()
+            for step in steps:
+                if step[0] == rotate_step and s == -2:
+                    right_tables()
+                if 0 <= s + step[1] < PAIRS:
+                    step[0](s + step[1], *step[2:])
+                if step[0] == widen:
+                    if s == -4:
+                        angles_2()
+                        nc.vector.tensor_copy(out=scale2[:, 1, :], in_=scale2[:, 0, :])
+                    if s == -3:
+                        latent_weights()
+                        expand_weights()
+                    if s == -2:
+                        gain_order()
+                if step[0] == quant_x and s == -3:
+                    split_left()

@@ -88,8 +88,8 @@ def tile_deepseekmultiheadattention_pb_t_w4_kernel(
         )
         ident = const.tile([P, P], F32)
         make_identity(nc, ident[:])
-        neg_half = const.tile([P, 2], F32)
-        nc.gpsimd.memset(neg_half[:], -0.5)
+        eps_col = const.tile([P, 1], F32)
+        nc.gpsimd.memset(eps_col[:], EPS)
         late = const.tile([P, 1], F32)
         nc.gpsimd.tensor_scalar(out=late[:], in0=pcol[:], scalar1=64.0, scalar2=None, op0=ALU.is_ge)
         t64 = const.tile([P, 1], F32)
@@ -202,10 +202,10 @@ def tile_deepseekmultiheadattention_pb_t_w4_kernel(
 
         def inverse_rms(j):
             ss = ss_sb[j]
-            ms = work.tile([P, 2], F32, name="ms")
-            nc.gpsimd.tensor_scalar(out=ms[:], in0=ss[:], scalar1=1.0 / LATENT, scalar2=EPS, op0=ALU.mult, op1=ALU.add)
             rs = work.tile([P, 2], F32, name="rs")
-            nc.gpsimd.tensor_tensor(out=rs[:], in0=ms[:], in1=neg_half[:], op=ALU.pow)
+            nc.scalar.activation(
+                out=rs[:], in_=ss[:], func=ACT.Abs_reciprocal_sqrt, scale=1.0 / LATENT, bias=eps_col[:]
+            )
             rms[j] = rs
 
         def normalise(j, t):
@@ -340,6 +340,7 @@ def tile_deepseekmultiheadattention_pb_t_w4_kernel(
             nc.vector.tensor_copy(out=trig_i[:], in_=trig[:])
             nc.vector.tensor_tensor(out=trig[:], in0=trig[:], in1=trig_i[:], op=ALU.subtract)
             nc.scalar.activation(out=trig[:], in_=trig[:], func=ACT.Sin, scale=2.0 * math.pi)
+            nc.scalar.activation(out=warm[:], in_=ones[:], func=ACT.Abs_reciprocal_sqrt)
 
         def split_left():
             s = trig[:, 0:512].rearrange("p (g q j) -> p g q j", g=GROUPS, q=2)
@@ -444,43 +445,41 @@ def tile_deepseekmultiheadattention_pb_t_w4_kernel(
             )
 
         steps = (
-            (widen, 4),
-            (latent, 2, 0),
-            (copy_x, 3),
-            (normalise, 1, 0),
-            (expand, -1),
-            (latent, 2, 1),
-            (normalise, 1, 1),
-            (transpose_cn, 1),
-            (squares, 2, 0),
-            (quant_cn, 0),
-            (quant_x, 3),
-            (rotate_step, 1),
-            (squares, 2, 1),
-            (copy_nope, -1),
-            (inverse_rms, 2),
-            (copy_v, -1),
-            (copy_cn, 1),
-            (transpose_x, 4),
+            (widen, 5),
+            (copy_x, 4),
+            (normalise, 2, 0),
+            (latent, 3, 0),
+            (expand, 0),
+            (squares, 3, 0),
+            (normalise, 2, 1),
+            (copy_v, 0),
+            (quant_x, 4),
+            (copy_nope, 0),
+            (latent, 3, 1),
+            (squares, 3, 1),
+            (transpose_cn, 2),
+            (copy_cn, 2),
+            (inverse_rms, 3),
+            (quant_cn, 1),
+            (transpose_x, 5),
+            (rotate_step, 2),
         )
-        for s in range(-4, PAIRS + 1):
-            if s == -4:
+        for s in range(-5, PAIRS + 1):
+            if s == -5:
                 angles()
-            if s == -2:
-                turn_tables()
+                angles_2()
             for step in steps:
-                if step[0] == rotate_step and s == -2:
-                    right_tables()
                 if 0 <= s + step[1] < PAIRS:
                     step[0](s + step[1], *step[2:])
                 if step[0] == widen:
-                    if s == -4:
-                        angles_2()
+                    if s == -5:
                         nc.vector.tensor_copy(out=scale2[:, 1, :], in_=scale2[:, 0, :])
-                    if s == -3:
+                    if s == -4:
                         latent_weights()
                         expand_weights()
-                    if s == -2:
+                        split_left()
+                    if s == -3:
+                        right_tables()
                         gain_order()
-                if step[0] == quant_x and s == -3:
-                    split_left()
+            if s == -4:
+                turn_tables()

@@ -34,7 +34,7 @@ def tile_deepseekmultiheadattention_pb_t_w4_kernel(
     nc = tc.nc
     with ExitStack() as ctx:
         const = ctx.enter_context(tc.tile_pool(name="const", bufs=1))
-        work = ctx.enter_context(tc.tile_pool(name="work", bufs=5))
+        work = ctx.enter_context(tc.tile_pool(name="work", bufs=8))
         outs = ctx.enter_context(tc.tile_pool(name="outs", bufs=3))
         psum = ctx.enter_context(tc.psum_pool(name="psum", bufs=1))
         ctx.enter_context(tc.manual_schedule())
@@ -55,8 +55,8 @@ def tile_deepseekmultiheadattention_pb_t_w4_kernel(
             nc.sync.dma_start(out=xb[:, a:b, :], in_=x_rows[:, a:b, :])
 
         load_x(0, 2)
-        scale2 = const.tile([P, 2, DIM], F32)
-        nc.sync.dma_start(out=scale2[:, 0, :], in_=x_scale.rearrange("a b k -> (a b k)").partition_broadcast(P))
+        scale_col = const.tile([P, 4], F32)
+        nc.sync.dma_start(out=scale_col[:], in_=x_scale.rearrange("a b (p t) -> p (a b t)", t=4))
         wc_nat = const.tile([P, 2 * LATENT], U8, align_bytes=64)
         nc.sync.dma_start(out=wc_nat[:].bitcast(I32), in_=wkv_c_words[0].bitcast(I32))
         for r in range(4):
@@ -142,21 +142,17 @@ def tile_deepseekmultiheadattention_pb_t_w4_kernel(
         v_ps, n_ps, v_sb, ks_sb = {}, {}, {}, {}
         t_ps, ss_sb = {}, {}
 
-        def widen(j):
+        def cast(j):
             xw = work.tile([P, 2, DIM], BF16, name="xw")
             x_bf[j] = xw
-            if j == 0:
-                for t in range(2):
-                    nc.vector.tensor_tensor(
-                        out=xw[:, t, :], in0=xb[:, t, :].bitcast(FP8), in1=scale2[:, 0, :], op=ALU.mult
-                    )
-            else:
-                nc.vector.tensor_tensor(
+            if j < 2:
+                nc.vector.tensor_copy(
                     out=xw[:].rearrange("p a k -> p (a k)"),
-                    in0=xb[:, 2 * j : 2 * j + 2, :].rearrange("p a k -> p (a k)").bitcast(FP8),
-                    in1=scale2[:].rearrange("p a k -> p (a k)"),
-                    op=ALU.mult,
+                    in_=xb[:, 2 * j : 2 * j + 2, :].rearrange("p a k -> p (a k)").bitcast(FP8),
                 )
+            else:
+                for t in range(2):
+                    nc.gpsimd.tensor_copy(out=xw[:, t, :], in_=xb[:, 2 * j + t, :].bitcast(FP8))
 
         def transpose_x(j):
             bank = psum.tile([P, 2, 2, P], F32, name="xt", tag="t", bufs=2)
@@ -164,14 +160,19 @@ def tile_deepseekmultiheadattention_pb_t_w4_kernel(
             for t in range(2):
                 words = x_bf[j][:, t, :].bitcast(F32)
                 for u in range(2):
-                    nc.tensor.transpose(bank[:, t, u, :], words[:, u:256:2], ident[:])
+                    nc.tensor.transpose(bank[:, u, t, :], words[:, u:256:2], ident[:])
 
-        def copy_x(j):
+        def scale_x(j):
             xg = work.tile([P, 8 * P], BF16, name="xg", align_bytes=64)
             x_grp[j] = xg
-            nc.scalar.copy(
-                out=xg[:].bitcast(F32).rearrange("p (a r u) -> p a r u", a=2, u=2),
-                in_=t_ps["x", j][:].rearrange("p a u r -> p a r u"),
+            nc.vector.tensor_tensor(
+                out=xg[:].rearrange("p (n u e) -> p n u e", u=2, e=2),
+                in0=t_ps["x", j][:]
+                .rearrange("p u a r -> p (u a r)")
+                .bitcast(BF16)
+                .rearrange("p (u n e) -> p n u e", u=2, e=2),
+                in1=scale_col[:].rearrange("p (u e) -> p u e", e=2).unsqueeze(1).to_broadcast([P, 2 * P, 2, 2]),
+                op=ALU.mult,
             )
 
         def quant_x(j):
@@ -383,36 +384,36 @@ def tile_deepseekmultiheadattention_pb_t_w4_kernel(
             nc.tensor.matmul(flat, left_rot[:, g, :], rot_lo[:], start=False, stop=True)
 
         def rotate_step(j):
-            if j % 4 == 0:
-                rotate_pe(j // 4)
-            rotate(j // 4, j % 4)
-            if j % 4 == 3:
-                turned.add(j // 4)
-                for q in (j // 2 - 1, j // 2):
+            g, part = j // 4, j % 4
+            if part == 0:
+                rotate_pe(g)
+                tab = work.tile([P, GROUP, 2, HALF], F32, name="tab", bufs=2)
+                nc.scalar.copy(out=tab[:], in_=r_ps[g][:])
+                r_ps[g] = tab
+                m_sb[g] = work.tile([P, GROUP, 2, 2, HALF], F32, name="m", bufs=2)
+            i0 = 2 * part
+            kin = kp[:, GROUP * g + i0 : GROUP * g + i0 + 2, :].rearrange("p i (h j) -> p i h j", h=2)
+            nc.gpsimd.tensor_tensor(
+                out=m_sb[g][:, i0 : i0 + 2, :, :, :],
+                in0=kin.unsqueeze(2).to_broadcast([P, 2, 2, 2, HALF]),
+                in1=r_ps[g][:, i0 : i0 + 2, :, :].unsqueeze(3).to_broadcast([P, 2, 2, 2, HALF]),
+                op=ALU.mult,
+            )
+            if part == 3:
+                ks, m = ks_tile(g), m_sb[g]
+                nc.gpsimd.tensor_tensor(
+                    out=ks[:, :, 2 * NOPE : 2 * NOPE + HALF],
+                    in0=m[:, :, 0, 0, :],
+                    in1=m[:, :, 1, 1, :],
+                    op=ALU.subtract,
+                )
+                nc.gpsimd.tensor_tensor(
+                    out=ks[:, :, 2 * NOPE + HALF :], in0=m[:, :, 0, 1, :], in1=m[:, :, 1, 0, :], op=ALU.add
+                )
+                turned.add(g)
+                for q in (2 * g, 2 * g + 1):
                     if q in have:
                         store_ks(q)
-
-        def rotate(g, phase):
-            kin = kp[:, GROUP * g : GROUP * (g + 1), :].rearrange("p i (h j) -> p i h j", h=2)
-            if phase < 2:
-                m = work.tile([P, GROUP, 2, HALF], F32, name="m%d" % phase, bufs=2)
-                m_sb[g, phase] = m
-                nc.vector.tensor_tensor(
-                    out=m[:],
-                    in0=kin,
-                    in1=r_ps[g][:, :, phase, :].unsqueeze(2).to_broadcast([P, GROUP, 2, HALF]),
-                    op=ALU.mult,
-                )
-            else:
-                other = phase == 2
-                ks = ks_tile(g)
-                c0 = 2 * NOPE + (0 if other else HALF)
-                nc.vector.tensor_tensor(
-                    out=ks[:, :, c0 : c0 + HALF],
-                    in0=m_sb[g, 0][:, :, 0 if other else 1, :],
-                    in1=m_sb[g, 1][:, :, 1 if other else 0, :],
-                    op=ALU.subtract if other else ALU.add,
-                )
 
         wc = const.tile([P, 2 * LATENT], U8, align_bytes=64)
         wcs = const.tile([P, LATENT], U8, align_bytes=64)
@@ -445,41 +446,39 @@ def tile_deepseekmultiheadattention_pb_t_w4_kernel(
             )
 
         steps = (
-            (widen, 5),
-            (copy_x, 4),
-            (normalise, 2, 0),
-            (latent, 3, 0),
-            (expand, 0),
-            (squares, 3, 0),
-            (normalise, 2, 1),
-            (copy_v, 0),
-            (quant_x, 4),
-            (copy_nope, 0),
-            (latent, 3, 1),
-            (squares, 3, 1),
-            (transpose_cn, 2),
-            (copy_cn, 2),
-            (inverse_rms, 3),
-            (quant_cn, 1),
+            (normalise, 0, 0),
+            (scale_x, 4),
+            (latent, 1, 0),
+            (expand, -3),
+            (cast, 6),
+            (latent, 1, 1),
+            (squares, 1, 0),
+            (transpose_cn, -1),
+            (copy_v, -3),
+            (squares, 1, 1),
+            (rotate_step, -1),
+            (normalise, 0, 1),
+            (quant_cn, -2),
+            (copy_nope, -3),
+            (inverse_rms, 1),
+            (quant_x, 3),
             (transpose_x, 5),
-            (rotate_step, 2),
+            (copy_cn, -1),
         )
-        for s in range(-5, PAIRS + 1):
-            if s == -5:
-                angles()
-                angles_2()
+        for s in range(-6, PAIRS + 4):
             for step in steps:
                 if 0 <= s + step[1] < PAIRS:
                     step[0](s + step[1], *step[2:])
-                if step[0] == widen:
+                if step[0] == cast:
+                    if s == -6:
+                        angles()
+                        angles_2()
                     if s == -5:
-                        nc.vector.tensor_copy(out=scale2[:, 1, :], in_=scale2[:, 0, :])
-                    if s == -4:
                         latent_weights()
                         expand_weights()
                         split_left()
-                    if s == -3:
+                    if s == -4:
                         right_tables()
                         gain_order()
-            if s == -4:
+            if s == -5:
                 turn_tables()

import math
from contextlib import ExitStack

import concourse.mybir as mybir
from concourse.masks import make_identity

F32 = mybir.dt.float32
BF16 = mybir.dt.bfloat16
I32 = mybir.dt.int32
U32 = mybir.dt.uint32
U8 = mybir.dt.uint8
FP8 = mybir.dt.float8_e4m3fn
FP8X4 = mybir.dt.float8_e4m3fn_x4
FP4X4 = mybir.dt.float4_e2m1fn_x4
ALU = mybir.AluOpType
ACT = mybir.ActivationFunctionType

P = 128
TOKENS, DIM, LATENT = 8192, 512, 512
HEADS, NOPE, ROPE, VDIM = 2, 64, 64, 128
HALF = ROPE // 2
EPS = 2.0**-23
TILES = TOKENS // P
PAIRS = TILES // 2
GROUP = 8
GROUPS = TILES // GROUP
KV = HEADS * (NOPE + VDIM)
FLOPS = 2 * TOKENS * DIM * (LATENT + KV)


def tile_deepseekmultiheadattention_pb_t_w4_kernel(
    tc, x_bytes, x_scale, wkv_c_words, wkv_c_scales, kv_a_norm_w, wkv_b_words, wkv_b_scales, k_pe, out_0, out_1
):
    nc = tc.nc
    with ExitStack() as ctx:
        const = ctx.enter_context(tc.tile_pool(name="const", bufs=1))
        work = ctx.enter_context(tc.tile_pool(name="work", bufs=8))
        outs = ctx.enter_context(tc.tile_pool(name="outs", bufs=3))
        psum = ctx.enter_context(tc.psum_pool(name="psum", bufs=1))
        ctx.enter_context(tc.manual_schedule())

        ones = const.tile([P, 1], F32)
        nc.vector.memset(ones[:], 1.0)
        warm = const.tile([P, 1], F32)
        nc.scalar.activation(out=warm[:], in_=ones[:], func=ACT.Sin)
        wc_scale_rows = const.tile([P, LATENT], U8, align_bytes=64)
        nc.vector.memset(wc_scale_rows[:].bitcast(I32), 0)
        wb_scale_rows = const.tile([P, KV], U8, align_bytes=64)
        nc.vector.memset(wb_scale_rows[:].bitcast(I32), 0)

        xb = const.tile([P, TILES, DIM], U8)
        x_rows = x_bytes[0].rearrange("(p i) k -> p i k", p=P)

        def load_x(a, b):
            nc.sync.dma_start(out=xb[:, a:b, :], in_=x_rows[:, a:b, :])

        load_x(0, 2)
        scale_col = const.tile([P, 4], F32)
        nc.sync.dma_start(out=scale_col[:], in_=x_scale.rearrange("a b (p t) -> p (a b t)", t=4))
        wc_nat = const.tile([P, 2 * LATENT], U8, align_bytes=64)
        nc.sync.dma_start(out=wc_nat[:].bitcast(I32), in_=wkv_c_words[0].bitcast(I32))
        for r in range(4):
            nc.sync.dma_start(out=wc_scale_rows[r:P:32, :].bitcast(I32), in_=wkv_c_scales[0][r:16:4, :].bitcast(I32))
        load_x(2, 8)
        gain_nat = const.tile([P, LATENT], BF16)
        nc.sync.dma_start(out=gain_nat[:], in_=kv_a_norm_w.partition_broadcast(P))
        wb = const.tile([P, 2 * KV], U8, align_bytes=64)
        wb_in = wkv_b_words[0].bitcast(I32).rearrange("p (h c) -> p h c", h=HEADS)
        wb_out = wb[:].bitcast(I32)
        nc.sync.dma_start(out=wb_out[:, 0:128].rearrange("p (h c) -> p h c", h=HEADS), in_=wb_in[:, :, 32:96])
        nc.sync.dma_start(out=wb_out[:, 128:192].rearrange("p (h c) -> p h c", h=HEADS), in_=wb_in[:, :, 0:32])
        for r in range(4):
            nc.sync.dma_start(out=wb_scale_rows[r:P:32, :].bitcast(I32), in_=wkv_b_scales[0][r:16:4, :].bitcast(I32))
        load_x(8, 16)
        kp = const.tile([P, TILES, ROPE], BF16)
        kp_rows = k_pe[0].rearrange("(p i) c -> p i c", p=P)
        nc.sync.dma_start(out=kp[:, 0:16, :], in_=kp_rows[:, 0:16, :])
        load_x(16, 24)
        nc.sync.dma_start(out=kp[:, 16:TILES, :], in_=kp_rows[:, 16:TILES, :])
        for a in range(24, TILES, 8):
            load_x(a, a + 8)

        pcol = const.tile([P, 1], F32)
        nc.gpsimd.iota(pcol[:], [[0, 1]], base=0, channel_multiplier=1, allow_small_or_imprecise_dtypes=True)
        eights = const.tile([P, GROUPS], F32)
        nc.gpsimd.iota(
            eights[:], [[GROUP, GROUPS]], base=0, channel_multiplier=0, allow_small_or_imprecise_dtypes=True
        )
        ident = const.tile([P, P], F32)
        make_identity(nc, ident[:])
        eps_col = const.tile([P, 1], F32)
        nc.gpsimd.memset(eps_col[:], EPS)
        late = const.tile([P, 1], F32)
        nc.gpsimd.tensor_scalar(out=late[:], in0=pcol[:], scalar1=64.0, scalar2=None, op0=ALU.is_ge)
        t64 = const.tile([P, 1], F32)
        nc.gpsimd.tensor_scalar(out=t64[:], in0=late[:], scalar1=-64.0, scalar2=0.0, op0=ALU.mult, op1=ALU.add)
        xi = const.tile([P, 1], F32)
        nc.gpsimd.tensor_tensor(out=xi[:], in0=pcol[:], in1=t64[:], op=ALU.add)
        ph0 = const.tile([P, 1], F32)
        nc.gpsimd.tensor_scalar(out=ph0[:], in0=late[:], scalar1=-0.25, scalar2=0.25, op0=ALU.mult, op1=ALU.add)
        sg1 = const.tile([P, 1], F32)
        nc.gpsimd.tensor_scalar(out=sg1[:], in0=late[:], scalar1=2.0, scalar2=-1.0, op0=ALU.mult, op1=ALU.add)
        xs = const.tile([P, 1], F32)
        nc.gpsimd.tensor_tensor(out=xs[:], in0=xi[:], in1=sg1[:], op=ALU.mult)
        ph1 = const.tile([P, 1], F32)
        nc.gpsimd.tensor_scalar(out=ph1[:], in0=late[:], scalar1=0.25, scalar2=0.0, op0=ALU.mult, op1=ALU.add)

        ratio = 10000.0 ** (-1.0 / HALF)
        freq = const.tile([P, HALF], F32)
        turn64 = const.tile([P, HALF], F32)
        nc.vector.tensor_scalar(
            out=freq[:, 0:1], in0=ones[:], scalar1=1.0 / (2.0 * math.pi), scalar2=None, op0=ALU.mult
        )
        filled = 1
        for j in range(HALF):
            turns = 64.0 * ratio**j / (2.0 * math.pi)
            turns = turns - round(turns)
            if j % 3 == 2:
                nc.scalar.activation(out=turn64[:, j : j + 1], in_=ones[:], func=ACT.Copy, scale=turns)
            else:
                nc.vector.tensor_scalar(
                    out=turn64[:, j : j + 1], in0=ones[:], scalar1=turns, scalar2=None, op0=ALU.mult
                )
            if j % 4 == 3 and filled < HALF:
                nc.vector.tensor_scalar(
                    out=freq[:, filled : 2 * filled], in0=freq[:, 0:filled], scalar1=ratio**filled, scalar2=None,
                    op0=ALU.mult,
                )
                filled *= 2
        step8 = const.tile([P, GROUPS, HALF], F32)
        nc.vector.tensor_tensor(
            out=step8[:],
            in0=freq[:].unsqueeze(1).to_broadcast([P, GROUPS, HALF]),
            in1=eights[:].unsqueeze(2).to_broadcast([P, GROUPS, HALF]),
            op=ALU.mult,
        )
        base = const.tile([P, HALF], F32)
        nc.vector.tensor_scalar(out=base[:], in0=turn64[:], scalar1=pcol[:], scalar2=None, op0=ALU.mult)

        x_bf, x_grp, x_cod, x_scl = {}, {}, {}, {}
        c_ps, rms, cn_bf, cn_cod, cn_scl = {}, {}, {}, {}, {}
        v_ps, n_ps, v_sb, ks_sb = {}, {}, {}, {}
        t_ps, ss_sb = {}, {}

        def cast(j):
            xw = work.tile([P, 2, DIM], BF16, name="xw")
            x_bf[j] = xw
            if j < 2:
                nc.vector.tensor_copy(
                    out=xw[:].rearrange("p a k -> p (a k)"),
                    in_=xb[:, 2 * j : 2 * j + 2, :].rearrange("p a k -> p (a k)").bitcast(FP8),
                )
            else:
                for t in range(2):
                    nc.gpsimd.tensor_copy(out=xw[:, t, :], in_=xb[:, 2 * j + t, :].bitcast(FP8))

        def transpose_x(j):
            bank = psum.tile([P, 2, 2, P], F32, name="xt", tag="t", bufs=2)
            t_ps["x", j] = bank
            for t in range(2):
                words = x_bf[j][:, t, :].bitcast(F32)
                for u in range(2):
                    nc.tensor.transpose(bank[:, u, t, :], words[:, u:256:2], ident[:])

        def scale_x(j):
            xg = work.tile([P, 8 * P], BF16, name="xg", align_bytes=64)
            x_grp[j] = xg
            nc.vector.tensor_tensor(
                out=xg[:].rearrange("p (n u e) -> p n u e", u=2, e=2),
                in0=t_ps["x", j][:]
                .rearrange("p u a r -> p (u a r)")
                .bitcast(BF16)
                .rearrange("p (u n e) -> p n u e", u=2, e=2),
                in1=scale_col[:].rearrange("p (u e) -> p u e", e=2).unsqueeze(1).to_broadcast([P, 2 * P, 2, 2]),
                op=ALU.mult,
            )

        def quant_x(j):
            cod = work.tile([P, 2 * P], U32, name="xq", align_bytes=64)
            scl = work.tile([P, 2 * P], U8, name="xqs", align_bytes=64)
            x_cod[j], x_scl[j] = cod, scl
            nc.vector.quantize_mx(out=cod[:].bitcast(FP8X4), scales=scl[:], in_=x_grp[j][:])

        def latent(j, t):
            bank = psum.tile([P, LATENT], F32, name="c", tag="c", bufs=3)
            c_ps[j, t] = bank
            cols = slice(t * P, (t + 1) * P)
            nc.tensor.matmul_mx(
                out=bank[:],
                lhsT=x_cod[j][:, cols].bitcast(FP8X4),
                lhsT_scale=x_scl[j][:, cols],
                rhs=wc[:].bitcast(FP4X4),
                rhs_scale=wcs[:],
                start=True,
                stop=True,
            )

        def squares(j, t):
            if t == 0:
                ss_sb[j] = work.tile([P, 2], F32, name="ss")
            junk = work.tile([P, LATENT], BF16, name="junk", bufs=2)
            nc.scalar.activation(out=junk[:], in_=c_ps[j, t][:], func=ACT.Square, accum_out=ss_sb[j][:, t : t + 1])

        def inverse_rms(j):
            ss = ss_sb[j]
            rs = work.tile([P, 2], F32, name="rs")
            nc.scalar.activation(
                out=rs[:], in_=ss[:], func=ACT.Abs_reciprocal_sqrt, scale=1.0 / LATENT, bias=eps_col[:]
            )
            rms[j] = rs

        def normalise(j, t):
            if t == 0:
                cn_bf[j] = work.tile([P, 2, LATENT], BF16, name="cn")
            nc.vector.scalar_tensor_tensor(
                out=cn_bf[j][:, t, :],
                in0=c_ps[j, t][:],
                scalar=rms[j][:, t : t + 1],
                in1=gain[:],
                op0=ALU.mult,
                op1=ALU.mult,
            )

        def transpose_cn(j):
            bank = psum.tile([P, 2, 2, P], F32, name="ct", tag="t", bufs=2)
            t_ps["c", j] = bank
            for t in range(2):
                words = cn_bf[j][:, t, :].bitcast(F32)
                for u in range(2):
                    nc.tensor.transpose(bank[:, t, u, :], words[:, u * P : (u + 1) * P], ident[:])

        def copy_cn(j):
            cg = work.tile([P, 8 * P], BF16, name="cg", align_bytes=64)
            cn_bf[j] = cg
            nc.scalar.copy(
                out=cg[:].bitcast(F32).rearrange("p (a r u) -> p a r u", a=2, u=2),
                in_=t_ps["c", j][:].rearrange("p a u r -> p a r u"),
            )

        def quant_cn(j):
            cod = work.tile([P, 2 * P], U32, name="cq", align_bytes=64)
            scl = work.tile([P, 2 * P], U8, name="cqs", align_bytes=64)
            cn_cod[j], cn_scl[j] = cod, scl
            nc.vector.quantize_mx(out=cod[:].bitcast(FP8X4), scales=scl[:], in_=cn_bf[j][:])

        def expand(j):
            v_ps[j] = psum.tile([P, 2, HEADS * VDIM], F32, name="v", tag="v")
            if j % 2 == 0:
                n_ps[j // 2] = psum.tile([P, 4, HEADS * NOPE], F32, name="n", tag="n")
            for t in range(2):
                cols = slice(t * P, (t + 1) * P)
                left = cn_cod[j][:, cols].bitcast(FP8X4)
                left_scale = cn_scl[j][:, cols]
                nc.tensor.matmul_mx(
                    out=v_ps[j][:, t, :],
                    lhsT=left,
                    lhsT_scale=left_scale,
                    rhs=wb[:, 0:512].bitcast(FP4X4),
                    rhs_scale=wbs[:, 0:256],
                    start=True,
                    stop=True,
                )
                nc.tensor.matmul_mx(
                    out=n_ps[j // 2][:, 2 * (j % 2) + t, :],
                    lhsT=left,
                    lhsT_scale=left_scale,
                    rhs=wb[:, 512:768].bitcast(FP4X4),
                    rhs_scale=wbs[:, 256:384],
                    start=True,
                    stop=True,
                )

        def ks_tile(g):
            if g not in ks_sb:
                ks_sb[g] = outs.tile([P, GROUP, 3 * ROPE], F32, name="ks")
            return ks_sb[g]

        def copy_v(j):
            q = j // 2
            if j % 2 == 0:
                v_sb[q] = outs.tile([P, HEADS, 4, VDIM], F32, name="vo")
            a = 2 * (j % 2)
            nc.scalar.copy(
                out=v_sb[q][:, :, a : a + 2, :].rearrange("p h i c -> p i h c"),
                in_=v_ps[j][:].rearrange("p i (h c) -> p i h c", h=HEADS),
            )
            v_rows = out_1[0].rearrange("h (p i) c -> p h i c", p=P)
            if q == PAIRS // 2 - 1:
                nc.sync.dma_start(
                    out=v_rows[:, :, 2 * j : 2 * j + 2, :], in_=v_sb[q][:, :, a : a + 2, :]
                )
            elif j % 2 == 1:
                nc.sync.dma_start(out=v_rows[:, :, 4 * q : 4 * q + 4, :], in_=v_sb[q][:])

        def store_ks(q):
            b = 4 * (q % 2)
            ks = ks_tile(q // 2)[:, b : b + 4, :]
            out0 = out_0[0, 0].rearrange("(p i) c -> p i c", p=P)[:, 4 * q : 4 * q + 4, :]
            out1 = out_0[0, 1].rearrange("(p i) c -> p i c", p=P)[:, 4 * q : 4 * q + 4, :]
            nc.sync.dma_start(out=out1, in_=ks[:, :, NOPE : 3 * NOPE])
            nc.sync.dma_start(out=out0[:, :, 0:NOPE], in_=ks[:, :, 0:NOPE])
            nc.sync.dma_start(out=out0[:, :, NOPE:], in_=ks[:, :, 2 * NOPE :])

        def copy_nope(j):
            if j % 2 == 1:
                q = j // 2
                b = 4 * (q % 2)
                nc.scalar.copy(out=ks_tile(q // 2)[:, b : b + 4, 0 : 2 * NOPE], in_=n_ps[q][:])
                have.add(q)
                if q // 2 in turned:
                    store_ks(q)

        trig = const.tile([P, 640], F32)
        trig_i = const.tile([P, 640], I32)
        lt = const.tile([P, GROUPS, 4, HALF], BF16)
        left_rot = const.tile([P, GROUPS, P], BF16)
        ident_b = const.tile([P, P], BF16)
        mask = const.tile([P, HALF], F32)
        rot_hi = const.tile([P, 2 * GROUP * HALF], BF16)
        rot_lo = const.tile([P, 2 * GROUP * HALF], BF16)
        rot = const.tile([P, 2 * GROUP * HALF], F32)
        short = const.tile([P, GROUP, 2], F32)

        def angles():
            u = trig[:, 0:512].rearrange("p (g q j) -> p g q j", g=GROUPS, q=2)
            nc.vector.tensor_tensor(
                out=u[:, :, 1, :], in0=step8[:], in1=base[:].unsqueeze(1).to_broadcast([P, GROUPS, HALF]), op=ALU.add
            )
            nc.vector.tensor_scalar(out=u[:, :, 0, :], in0=u[:, :, 1, :], scalar1=0.25, scalar2=None, op0=ALU.add)

        def angles_2():
            for q in range(4):
                nc.vector.tensor_scalar(
                    out=trig[:, 512 + HALF * q : 512 + HALF * (q + 1)],
                    in0=freq[:],
                    scalar1=(xs if q % 2 else xi)[:],
                    scalar2=(ph1 if q % 2 else ph0)[:],
                    op0=ALU.mult,
                    op1=ALU.add,
                )
            nc.vector.tensor_copy(out=trig_i[:], in_=trig[:])
            nc.vector.tensor_tensor(out=trig[:], in0=trig[:], in1=trig_i[:], op=ALU.subtract)
            nc.scalar.activation(out=trig[:], in_=trig[:], func=ACT.Sin, scale=2.0 * math.pi)
            nc.scalar.activation(out=warm[:], in_=ones[:], func=ACT.Abs_reciprocal_sqrt)

        def split_left():
            s = trig[:, 0:512].rearrange("p (g q j) -> p g q j", g=GROUPS, q=2)
            nc.vector.tensor_copy(out=ident_b[:], in_=ident[:])
            nc.vector.tensor_copy(out=lt[:, :, 0:2, :], in_=s)
            nc.vector.tensor_tensor(out=lt[:, :, 2:4, :], in0=s, in1=lt[:, :, 0:2, :], op=ALU.subtract)
            nc.vector.tensor_reduce(
                out=mask[:], in_=ident[:].rearrange("k (q j) -> k j q", q=4), axis=mybir.AxisListType.X, op=ALU.add
            )

        def turn_tables():
            xt = psum.tile([P, P], F32, name="tx", tag="v")
            nc.tensor.transpose(xt[:], trig[:, 512:640], ident[:])
            bank = psum.tile([P, GROUPS, P], BF16, name="tl", tag="r")
            for g in range(GROUPS):
                nc.tensor.transpose(bank[:, g, :], lt[:, g, :, :].rearrange("p q j -> p (q j)"), ident_b[:])
            nc.vector.tensor_copy(
                out=short[:], in_=xt[:].rearrange("k (c i) -> k i c", c=2)[:, 0:GROUP, :]
            )
            nc.scalar.copy(out=left_rot[:], in_=bank[:])

        def right_tables():
            nc.vector.tensor_tensor(
                out=rot[:].rearrange("k (i c j) -> k i c j", i=GROUP, c=2),
                in0=short[:].unsqueeze(3).to_broadcast([P, GROUP, 2, HALF]),
                in1=mask[:].unsqueeze(1).unsqueeze(1).to_broadcast([P, GROUP, 2, HALF]),
                op=ALU.mult,
            )
            nc.vector.tensor_copy(out=rot_hi[:], in_=rot[:])
            nc.vector.tensor_tensor(out=rot_lo[:], in0=rot[:], in1=rot_hi[:], op=ALU.subtract)

        r_ps, m_sb = {}, {}
        have, turned = set(), set()

        def rotate_pe(g):
            bank = psum.tile([P, GROUP, 2, HALF], F32, name="r", tag="r")
            r_ps[g] = bank
            flat = bank[:].rearrange("p i c j -> p (i c j)")
            nc.tensor.matmul(flat, left_rot[:, g, :], rot_hi[:], start=True, stop=False)
            nc.tensor.matmul(flat, left_rot[:, g, :], rot_lo[:], start=False, stop=True)

        def rotate_step(j):
            g, part = j // 4, j % 4
            if part == 0:
                rotate_pe(g)
                tab = work.tile([P, GROUP, 2, HALF], F32, name="tab", bufs=2)
                nc.scalar.copy(out=tab[:], in_=r_ps[g][:])
                r_ps[g] = tab
                m_sb[g] = work.tile([P, GROUP, 2, 2, HALF], F32, name="m", bufs=2)
            i0 = 2 * part
            kin = kp[:, GROUP * g + i0 : GROUP * g + i0 + 2, :].rearrange("p i (h j) -> p i h j", h=2)
            nc.gpsimd.tensor_tensor(
                out=m_sb[g][:, i0 : i0 + 2, :, :, :],
                in0=kin.unsqueeze(2).to_broadcast([P, 2, 2, 2, HALF]),
                in1=r_ps[g][:, i0 : i0 + 2, :, :].unsqueeze(3).to_broadcast([P, 2, 2, 2, HALF]),
                op=ALU.mult,
            )
            if part == 3:
                ks, m = ks_tile(g), m_sb[g]
                nc.gpsimd.tensor_tensor(
                    out=ks[:, :, 2 * NOPE : 2 * NOPE + HALF],
                    in0=m[:, :, 0, 0, :],
                    in1=m[:, :, 1, 1, :],
                    op=ALU.subtract,
                )
                nc.gpsimd.tensor_tensor(
                    out=ks[:, :, 2 * NOPE + HALF :], in0=m[:, :, 0, 1, :], in1=m[:, :, 1, 0, :], op=ALU.add
                )
                turned.add(g)
                for q in (2 * g, 2 * g + 1):
                    if q in have:
                        store_ks(q)

        wc = const.tile([P, 2 * LATENT], U8, align_bytes=64)
        wcs = const.tile([P, LATENT], U8, align_bytes=64)
        wbs = const.tile([P, KV], U8, align_bytes=64)
        gain = const.tile([P, LATENT], BF16)

        def latent_weights():
            nc.vector.tensor_copy(
                out=wc[:].bitcast(I32).rearrange("q (u p) -> q p u", u=2),
                in_=wc_nat[:].bitcast(I32).rearrange("q (p u) -> q p u", u=2),
            )
            nc.vector.tensor_copy(
                out=wcs[:].rearrange("q (u p e) -> q p u e", u=2, e=2),
                in_=wc_scale_rows[:].rearrange("q (p u e) -> q p u e", u=2, e=2),
            )

        def gain_order():
            nc.vector.tensor_copy(
                out=gain[:].rearrange("q (u p e) -> q p u e", u=2, e=2),
                in_=gain_nat[:].rearrange("q (p u e) -> q p u e", u=2, e=2),
            )

        def expand_weights():
            rows = wb_scale_rows[:].rearrange("q (h c) -> q h c", h=HEADS)
            nc.gpsimd.tensor_copy(
                out=wbs[:, 0:256].rearrange("q (h c) -> q h c", h=HEADS), in_=rows[:, :, NOPE:]
            )
            nc.gpsimd.tensor_copy(
                out=wbs[:, 256:384].rearrange("q (h c) -> q h c", h=HEADS), in_=rows[:, :, 0:NOPE]
            )

        steps = (
            (normalise, 0, 0),
            (scale_x, 4),
            (latent, 1, 0),
            (expand, -3),
            (cast, 6),
            (latent, 1, 1),
            (squares, 1, 0),
            (transpose_cn, -1),
            (copy_v, -3),
            (squares, 1, 1),
            (rotate_step, -1),
            (normalise, 0, 1),
            (quant_cn, -2),
            (copy_nope, -3),
            (inverse_rms, 1),
            (quant_x, 3),
            (transpose_x, 5),
            (copy_cn, -1),
        )
        for s in range(-6, PAIRS + 4):
            for step in steps:
                if 0 <= s + step[1] < PAIRS:
                    step[0](s + step[1], *step[2:])
                if step[0] == cast:
                    if s == -6:
                        angles()
                        angles_2()
                    if s == -5:
                        latent_weights()
                        expand_weights()
                        split_left()
                    if s == -4:
                        right_tables()
                        gain_order()
            if s == -5:
                turn_tables()
